import numpy as np
import ml_dtypes


def mxq(x, axis, fmt="e4m3"):
    dtype, down = {"e4m3": (ml_dtypes.float8_e4m3fn, 7), "e5m2": (ml_dtypes.float8_e5m2, 14)}[fmt]
    v = np.moveaxis(np.asarray(x, np.float32).astype(ml_dtypes.bfloat16).astype(np.float64), axis, -1)
    blocks = v.reshape(v.shape[:-1] + (-1, 32))
    amax = np.abs(blocks).max(-1, keepdims=True)
    byte = np.maximum(np.where(amax > 0, np.frexp(amax)[1] - 1 + 127, 0) - down, 1)
    scale = np.exp2(byte - 127.0)
    codes = (blocks / scale).astype(np.float32).astype(dtype).astype(np.float64)
    return np.moveaxis((codes * scale).reshape(v.shape), -1, axis)


WIDE = False


def mx_kscale(k):
    if not WIDE:
        return np.ones(k)
    levels = np.array([10, -10, 5, -5, 0])
    a = np.random.permutation(np.resize(levels, k // 512 * 4)).reshape(k // 512, 4)
    idx = np.arange(k)
    return np.exp2(a[idx // 512, idx % 128 // 32])


BF16 = ml_dtypes.bfloat16


def bf(x):
    return np.asarray(x, np.float32).astype(BF16)


def f64(x):
    return np.asarray(x).astype(np.float64)


B, S, H, D, M = 2, 64, 16, 64, 1024
E = H * D
R = B * S
EPS = 1e-6


def setup_inputs():
    s = mx_kscale(E)
    return {"query_input": bf(np.random.standard_normal((B, S, E))),
            "norm_query_w": bf((1.0 + 0.1 * np.random.standard_normal(E)) * s),
            "W_in": bf(np.random.standard_normal((E, E)) / np.sqrt(E) / s[None, :])}


def reference(query_input, norm_query_w, W_in):
    x = f64(query_input).reshape(R, E)
    normed = x * (1.0 / np.sqrt(np.mean(x * x, 1, keepdims=True) + EPS))
    h = normed * f64(norm_query_w)
    return (mxq(h, 1, "e4m3") @ mxq(f64(W_in), 1, "e4m3").T).reshape(B, S, E)

@@ -1,0 +1,175 @@
+from contextlib import ExitStack
+
+import concourse.mybir as mybir
+from concourse.masks import make_identity
+
+F32 = mybir.dt.float32
+BF16 = mybir.dt.bfloat16
+U32 = mybir.dt.uint32
+U8 = mybir.dt.uint8
+FP8X4 = mybir.dt.float8_e4m3fn_x4
+ACT = mybir.ActivationFunctionType
+ALU = mybir.AluOpType
+
+P = 128
+E = 1024
+EPS = 1e-6
+PACK = 4
+PASSES = E // (P * PACK)
+WORDS = 2 * PASSES
+CHUNKS = E // P
+HEAD_CHUNKS = 2
+PAIR = 2 * P
+
+FLOPS = 2 * P * E * E
+
+
+def tile_hopfieldmemorylayer_pa_s_kernel(tc, query_input, norm_query_w, W_in, out):
+    nc = tc.nc
+    x_dram = query_input.flatten_outer_dims()
+    out_dram = out.flatten_outer_dims()
+
+    with ExitStack() as ctx:
+        keep = ctx.enter_context(tc.tile_pool(name="keep", bufs=1))
+        w_pool = ctx.enter_context(tc.tile_pool(name="w_rows", bufs=CHUNKS))
+        grouped_pool = ctx.enter_context(tc.tile_pool(name="grouped", bufs=3))
+        psum_w = ctx.enter_context(tc.psum_pool(name="psum_w", bufs=4))
+        psum_misc = ctx.enter_context(tc.psum_pool(name="psum_misc", bufs=4))
+
+        x_sb = keep.tile([P, E], BF16)
+        nc.sync.dma_start(out=x_sb[:], in_=x_dram)
+
+        g_rows = keep.tile([P, 2 * P], BF16)
+        nc.vector.memset(g_rows[:], 0.0)
+        nc.scalar.dma_start(
+            out=g_rows[0:WORDS, :], in_=norm_query_w.rearrange("(j c) -> j c", j=WORDS)
+        )
+
+        w_rows = []
+        for c in range(CHUNKS):
+            rows = w_pool.tile([P, E], BF16, name="rows", tag="rows")
+            nc.sync.dma_start(out=rows[:], in_=W_in[c * P : (c + 1) * P, :])
+            w_rows.append(rows)
+
+        identity = keep.tile([P, P], F32)
+        make_identity(nc, identity[:])
+
+        eps = keep.tile([P, 1], F32)
+        nc.vector.memset(eps[:], EPS)
+        table_warmer = keep.tile([P, 1], F32)
+        nc.scalar.activation(out=table_warmer[:], in_=eps[:], func=ACT.Sqrt)
+
+        g_t = psum_misc.tile([P, P], F32, tag="bank")
+        nc.tensor.transpose(g_t[:], g_rows[:].bitcast(F32), identity[:])
+        g_pairs = keep.tile([P, WORDS], F32)
+        nc.vector.tensor_copy(out=g_pairs[:], in_=g_t[:, 0:WORDS])
+        g_values = g_pairs[:].bitcast(BF16)
+
+        x_t = psum_misc.tile([P, WORDS, P], F32, tag="bank")
+        x_words = x_sb[:].bitcast(F32)
+        for j in range(WORDS):
+            nc.tensor.transpose(x_t[:, j, :], x_words[:, j * P : (j + 1) * P], identity[:])
+
+        squares = keep.tile([P, E], BF16)
+        sum_squares = keep.tile([P, 1], F32)
+        nc.scalar.activation(
+            out=squares[:], in_=x_sb[:], func=ACT.Square, accum_out=sum_squares[:]
+        )
+        rms = keep.tile([P, 1], F32)
+        nc.scalar.activation(
+            out=rms[:], in_=sum_squares[:], func=ACT.Sqrt, scale=1.0 / E, bias=eps[:]
+        )
+        inv_rms = keep.tile([P, 1], F32)
+
+        xg = keep.tile([P, PASSES, P, PACK], F32)
+
+        def gain(s):
+            nc.vector.tensor_tensor(
+                out=xg[:, s, :, :].rearrange("p r (u e) -> p r u e", e=2),
+                in0=x_t[:, 2 * s : 2 * s + 2, :]
+                .bitcast(BF16)
+                .rearrange("p u (r e) -> p r u e", e=2),
+                in1=g_values[:, PACK * s : PACK * (s + 1)]
+                .rearrange("p (u e) -> p u e", e=2)
+                .unsqueeze(1)
+                .to_broadcast([P, P, 2, 2]),
+                op=ALU.mult,
+            )
+
+        gain(0)
+        nc.vector.reciprocal(out=inv_rms[:], in_=rms[:])
+        gain(1)
+
+        w_codes = keep.tile([P, CHUNKS, PASSES * P], U32, align_bytes=64)
+        w_scales = keep.tile([P, CHUNKS, PASSES * P], U8, align_bytes=64)
+        w_grouped = {}
+
+        def transpose_chunk(c):
+            w_t = psum_w.tile([P, WORDS, P], F32, name="w_t", tag="w_t")
+            words = w_rows[c][:].bitcast(F32)
+            for j in range(WORDS):
+                nc.tensor.transpose(w_t[:, j, :], words[:, j * P : (j + 1) * P], identity[:])
+            grouped = grouped_pool.tile(
+                [P, PASSES, P, PACK], BF16, name="grouped", tag="grouped", align_bytes=64
+            )
+            nc.scalar.copy(
+                out=grouped[:].bitcast(F32),
+                in_=w_t[:].rearrange("p (s u) o -> p s o u", u=2),
+            )
+            w_grouped[c] = grouped
+
+        def quantise_chunk(c):
+            nc.vector.quantize_mx(
+                out=w_codes[:, c, :].bitcast(FP8X4),
+                scales=w_scales[:, c, :],
+                in_=w_grouped[c][:].rearrange("p s o t -> p (s o t)"),
+            )
+
+        for c in range(HEAD_CHUNKS):
+            transpose_chunk(c)
+
+        inv_rms_t = psum_misc.tile([P, P], F32, tag="bank")
+        nc.tensor.transpose(inv_rms_t[:], inv_rms[:, 0:1].to_broadcast([P, P]), identity[:])
+        h_grouped = keep.tile([P, PASSES, P, PACK], BF16, align_bytes=64)
+        nc.vector.tensor_tensor(
+            out=h_grouped[:],
+            in0=xg[:],
+            in1=inv_rms_t[:].unsqueeze(1).unsqueeze(3).to_broadcast([P, PASSES, P, PACK]),
+            op=ALU.mult,
+        )
+        h_codes = keep.tile([P, PASSES * P], U32, align_bytes=64)
+        h_scales = keep.tile([P, PASSES * P], U8, align_bytes=64)
+        nc.vector.quantize_mx(
+            out=h_codes[:].bitcast(FP8X4),
+            scales=h_scales[:],
+            in_=h_grouped[:].rearrange("p s r t -> p (s r t)"),
+        )
+
+        for c in range(HEAD_CHUNKS):
+            quantise_chunk(c)
+        for c in range(HEAD_CHUNKS, CHUNKS):
+            transpose_chunk(c)
+            quantise_chunk(c)
+
+        out_sb = keep.tile([P, E], F32)
+        for pair in range(E // PAIR):
+            acc = psum_misc.tile([P, PAIR], F32, tag="bank")
+            for half in range(2):
+                c = 2 * pair + half
+                for s in range(PASSES):
+                    k_cols = slice(s * P, (s + 1) * P)
+                    nc.tensor.matmul_mx(
+                        out=acc[:, half * P : (half + 1) * P],
+                        lhsT=h_codes[:, k_cols].bitcast(FP8X4),
+                        lhsT_scale=h_scales[:, k_cols],
+                        rhs=w_codes[:, c, k_cols].bitcast(FP8X4),
+                        rhs_scale=w_scales[:, c, k_cols],
+                        start=(s == 0),
+                        stop=(s == PASSES - 1),
+                    )
+            cols = slice(pair * PAIR, (pair + 1) * PAIR)
+            if pair % 2 == 0:
+                nc.vector.tensor_copy(out=out_sb[:, cols], in_=acc[:])
+            else:
+                nc.scalar.copy(out=out_sb[:, cols], in_=acc[:])
+            nc.sync.dma_start(out=out_dram[:, cols], in_=out_sb[:, cols])

@@ -32,9 +32,10 @@ def tile_hopfieldmemorylayer_pa_s_kernel(tc, query_input, norm_query_w, W_in, ou
     with ExitStack() as ctx:
         keep = ctx.enter_context(tc.tile_pool(name="keep", bufs=1))
         w_pool = ctx.enter_context(tc.tile_pool(name="w_rows", bufs=CHUNKS))
-        grouped_pool = ctx.enter_context(tc.tile_pool(name="grouped", bufs=3))
+        grouped_pool = ctx.enter_context(tc.tile_pool(name="grouped", bufs=CHUNKS))
         psum_w = ctx.enter_context(tc.psum_pool(name="psum_w", bufs=4))
         psum_misc = ctx.enter_context(tc.psum_pool(name="psum_misc", bufs=4))
+        ctx.enter_context(tc.manual_schedule())
 
         x_sb = keep.tile([P, E], BF16)
         nc.sync.dma_start(out=x_sb[:], in_=x_dram)
@@ -168,7 +169,7 @@ def tile_hopfieldmemorylayer_pa_s_kernel(tc, query_input, norm_query_w, W_in, ou
                         stop=(s == PASSES - 1),
                     )
             cols = slice(pair * PAIR, (pair + 1) * PAIR)
-            if pair % 2 == 0:
+            if pair == E // PAIR - 1:
                 nc.vector.tensor_copy(out=out_sb[:, cols], in_=acc[:])
             else:
                 nc.scalar.copy(out=out_sb[:, cols], in_=acc[:])

@@ -20,6 +20,7 @@ WORDS = 2 * PASSES
 CHUNKS = E // P
 HEAD_CHUNKS = 2
 PAIR = 2 * P
+HALF = E // 2
 
 FLOPS = 2 * P * E * E
 
@@ -39,10 +40,9 @@ def tile_hopfieldmemorylayer_pa_s_kernel(tc, query_input, norm_query_w, W_in, ou
 
         x_sb = keep.tile([P, E], BF16)
         nc.sync.dma_start(out=x_sb[:], in_=x_dram)
-
         g_rows = keep.tile([P, 2 * P], BF16)
         nc.vector.memset(g_rows[:], 0.0)
-        nc.scalar.dma_start(
+        nc.sync.dma_start(
             out=g_rows[0:WORDS, :], in_=norm_query_w.rearrange("(j c) -> j c", j=WORDS)
         )
 
@@ -60,28 +60,43 @@ def tile_hopfieldmemorylayer_pa_s_kernel(tc, query_input, norm_query_w, W_in, ou
         table_warmer = keep.tile([P, 1], F32)
         nc.scalar.activation(out=table_warmer[:], in_=eps[:], func=ACT.Sqrt)
 
-        g_t = psum_misc.tile([P, P], F32, tag="bank")
-        nc.tensor.transpose(g_t[:], g_rows[:].bitcast(F32), identity[:])
-        g_pairs = keep.tile([P, WORDS], F32)
-        nc.vector.tensor_copy(out=g_pairs[:], in_=g_t[:, 0:WORDS])
-        g_values = g_pairs[:].bitcast(BF16)
-
         x_t = psum_misc.tile([P, WORDS, P], F32, tag="bank")
         x_words = x_sb[:].bitcast(F32)
         for j in range(WORDS):
             nc.tensor.transpose(x_t[:, j, :], x_words[:, j * P : (j + 1) * P], identity[:])
 
-        squares = keep.tile([P, E], BF16)
-        sum_squares = keep.tile([P, 1], F32)
+        g_t = psum_misc.tile([P, P], F32, tag="bank")
+        nc.tensor.transpose(g_t[:], g_rows[:].bitcast(F32), identity[:])
+
+        squares_a = keep.tile([P, HALF], F32)
+        sum_a = keep.tile([P, 1], F32)
         nc.scalar.activation(
-            out=squares[:], in_=x_sb[:], func=ACT.Square, accum_out=sum_squares[:]
+            out=squares_a[:], in_=x_sb[:, 0:HALF], func=ACT.Square, accum_out=sum_a[:]
+        )
+        squares_b = keep.tile([P, HALF], F32)
+        sum_b = keep.tile([P, 1], F32)
+        nc.vector.scalar_tensor_tensor(
+            out=squares_b[:],
+            in0=x_sb[:, HALF:E],
+            scalar=1.0,
+            in1=x_sb[:, HALF:E],
+            op0=ALU.mult,
+            op1=ALU.mult,
+            accum_out=sum_b[:],
+        )
+        mean_b_eps = keep.tile([P, 1], F32)
+        nc.vector.tensor_scalar(
+            out=mean_b_eps[:], in0=sum_b[:], scalar1=1.0 / E, scalar2=EPS, op0=ALU.mult, op1=ALU.add
         )
         rms = keep.tile([P, 1], F32)
         nc.scalar.activation(
-            out=rms[:], in_=sum_squares[:], func=ACT.Sqrt, scale=1.0 / E, bias=eps[:]
+            out=rms[:], in_=sum_a[:], func=ACT.Sqrt, scale=1.0 / E, bias=mean_b_eps[:]
         )
         inv_rms = keep.tile([P, 1], F32)
 
+        g_pairs = keep.tile([P, WORDS], F32)
+        nc.vector.tensor_copy(out=g_pairs[:], in_=g_t[:, 0:WORDS])
+        g_values = g_pairs[:].bitcast(BF16)
         xg = keep.tile([P, PASSES, P, PACK], F32)
 
         def gain(s):

@@ -21,6 +21,8 @@ CHUNKS = E // P
 HEAD_CHUNKS = 2
 PAIR = 2 * P
 HALF = E // 2
+HEAD_WARM_UP = 16
+STREAM_WARM_UP = 6
 
 FLOPS = 2 * P * E * E
 
@@ -59,6 +61,25 @@ def tile_hopfieldmemorylayer_pa_s_kernel(tc, query_input, norm_query_w, W_in, ou
         nc.vector.memset(eps[:], EPS)
         table_warmer = keep.tile([P, 1], F32)
         nc.scalar.activation(out=table_warmer[:], in_=eps[:], func=ACT.Sqrt)
+
+        idle_values = keep.tile([P, PACK * P], BF16, align_bytes=64)
+        nc.vector.memset(idle_values[:], 0.0)
+        idle_codes = keep.tile([P, P], U32, align_bytes=64)
+        idle_scales = keep.tile([P, P], U8, align_bytes=64)
+        nc.vector.quantize_mx(
+            out=idle_codes[:].bitcast(FP8X4), scales=idle_scales[:], in_=idle_values[:]
+        )
+        idle_bank = psum_misc.tile([P, P], F32, tag="bank")
+        for i in range(HEAD_WARM_UP):
+            nc.tensor.matmul_mx(
+                out=idle_bank[:],
+                lhsT=idle_codes[:].bitcast(FP8X4),
+                lhsT_scale=idle_scales[:],
+                rhs=idle_codes[:].bitcast(FP8X4),
+                rhs_scale=idle_scales[:],
+                start=True,
+                stop=True,
+            )
 
         x_t = psum_misc.tile([P, WORDS, P], F32, tag="bank")
         x_words = x_sb[:].bitcast(F32)
@@ -125,6 +146,10 @@ def tile_hopfieldmemorylayer_pa_s_kernel(tc, query_input, norm_query_w, W_in, ou
             words = w_rows[c][:].bitcast(F32)
             for j in range(WORDS):
                 nc.tensor.transpose(w_t[:, j, :], words[:, j * P : (j + 1) * P], identity[:])
+            if c < STREAM_WARM_UP:
+                nc.tensor.matmul(
+                    out=idle_bank[:], lhsT=identity[:], rhs=identity[:], start=True, stop=True
+                )
             grouped = grouped_pool.tile(
                 [P, PASSES, P, PACK], BF16, name="grouped", tag="grouped", align_bytes=64
             )

from contextlib import ExitStack

import concourse.mybir as mybir
from concourse.masks import make_identity

F32 = mybir.dt.float32
BF16 = mybir.dt.bfloat16
U32 = mybir.dt.uint32
U8 = mybir.dt.uint8
FP8X4 = mybir.dt.float8_e4m3fn_x4
ACT = mybir.ActivationFunctionType
ALU = mybir.AluOpType

P = 128
E = 1024
EPS = 1e-6
PACK = 4
PASSES = E // (P * PACK)
WORDS = 2 * PASSES
CHUNKS = E // P
HEAD_CHUNKS = 2
PAIR = 2 * P
HALF = E // 2
HEAD_WARM_UP = 16
STREAM_WARM_UP = 6

FLOPS = 2 * P * E * E


def tile_hopfieldmemorylayer_pa_s_kernel(tc, query_input, norm_query_w, W_in, out):
    nc = tc.nc
    x_dram = query_input.flatten_outer_dims()
    out_dram = out.flatten_outer_dims()

    with ExitStack() as ctx:
        keep = ctx.enter_context(tc.tile_pool(name="keep", bufs=1))
        w_pool = ctx.enter_context(tc.tile_pool(name="w_rows", bufs=CHUNKS))
        grouped_pool = ctx.enter_context(tc.tile_pool(name="grouped", bufs=CHUNKS))
        psum_w = ctx.enter_context(tc.psum_pool(name="psum_w", bufs=4))
        psum_misc = ctx.enter_context(tc.psum_pool(name="psum_misc", bufs=4))
        ctx.enter_context(tc.manual_schedule())

        x_sb = keep.tile([P, E], BF16)
        nc.sync.dma_start(out=x_sb[:], in_=x_dram)
        g_rows = keep.tile([P, 2 * P], BF16)
        nc.vector.memset(g_rows[:], 0.0)
        nc.sync.dma_start(
            out=g_rows[0:WORDS, :], in_=norm_query_w.rearrange("(j c) -> j c", j=WORDS)
        )

        w_rows = []
        for c in range(CHUNKS):
            rows = w_pool.tile([P, E], BF16, name="rows", tag="rows")
            nc.sync.dma_start(out=rows[:], in_=W_in[c * P : (c + 1) * P, :])
            w_rows.append(rows)

        identity = keep.tile([P, P], F32)
        make_identity(nc, identity[:])

        eps = keep.tile([P, 1], F32)
        nc.vector.memset(eps[:], EPS)
        table_warmer = keep.tile([P, 1], F32)
        nc.scalar.activation(out=table_warmer[:], in_=eps[:], func=ACT.Sqrt)

        idle_values = keep.tile([P, PACK * P], BF16, align_bytes=64)
        nc.vector.memset(idle_values[:], 0.0)
        idle_codes = keep.tile([P, P], U32, align_bytes=64)
        idle_scales = keep.tile([P, P], U8, align_bytes=64)
        nc.vector.quantize_mx(
            out=idle_codes[:].bitcast(FP8X4), scales=idle_scales[:], in_=idle_values[:]
        )
        idle_bank = psum_misc.tile([P, P], F32, tag="bank")
        for i in range(HEAD_WARM_UP):
            nc.tensor.matmul_mx(
                out=idle_bank[:],
                lhsT=idle_codes[:].bitcast(FP8X4),
                lhsT_scale=idle_scales[:],
                rhs=idle_codes[:].bitcast(FP8X4),
                rhs_scale=idle_scales[:],
                start=True,
                stop=True,
            )

        x_t = psum_misc.tile([P, WORDS, P], F32, tag="bank")
        x_words = x_sb[:].bitcast(F32)
        for j in range(WORDS):
            nc.tensor.transpose(x_t[:, j, :], x_words[:, j * P : (j + 1) * P], identity[:])

        g_t = psum_misc.tile([P, P], F32, tag="bank")
        nc.tensor.transpose(g_t[:], g_rows[:].bitcast(F32), identity[:])

        squares_a = keep.tile([P, HALF], F32)
        sum_a = keep.tile([P, 1], F32)
        nc.scalar.activation(
            out=squares_a[:], in_=x_sb[:, 0:HALF], func=ACT.Square, accum_out=sum_a[:]
        )
        squares_b = keep.tile([P, HALF], F32)
        sum_b = keep.tile([P, 1], F32)
        nc.vector.scalar_tensor_tensor(
            out=squares_b[:],
            in0=x_sb[:, HALF:E],
            scalar=1.0,
            in1=x_sb[:, HALF:E],
            op0=ALU.mult,
            op1=ALU.mult,
            accum_out=sum_b[:],
        )
        mean_b_eps = keep.tile([P, 1], F32)
        nc.vector.tensor_scalar(
            out=mean_b_eps[:], in0=sum_b[:], scalar1=1.0 / E, scalar2=EPS, op0=ALU.mult, op1=ALU.add
        )
        rms = keep.tile([P, 1], F32)
        nc.scalar.activation(
            out=rms[:], in_=sum_a[:], func=ACT.Sqrt, scale=1.0 / E, bias=mean_b_eps[:]
        )
        inv_rms = keep.tile([P, 1], F32)

        g_pairs = keep.tile([P, WORDS], F32)
        nc.vector.tensor_copy(out=g_pairs[:], in_=g_t[:, 0:WORDS])
        g_values = g_pairs[:].bitcast(BF16)
        xg = keep.tile([P, PASSES, P, PACK], F32)

        def gain(s):
            nc.vector.tensor_tensor(
                out=xg[:, s, :, :].rearrange("p r (u e) -> p r u e", e=2),
                in0=x_t[:, 2 * s : 2 * s + 2, :]
                .bitcast(BF16)
                .rearrange("p u (r e) -> p r u e", e=2),
                in1=g_values[:, PACK * s : PACK * (s + 1)]
                .rearrange("p (u e) -> p u e", e=2)
                .unsqueeze(1)
                .to_broadcast([P, P, 2, 2]),
                op=ALU.mult,
            )

        gain(0)
        nc.vector.reciprocal(out=inv_rms[:], in_=rms[:])
        gain(1)

        w_codes = keep.tile([P, CHUNKS, PASSES * P], U32, align_bytes=64)
        w_scales = keep.tile([P, CHUNKS, PASSES * P], U8, align_bytes=64)
        w_grouped = {}

        def transpose_chunk(c):
            w_t = psum_w.tile([P, WORDS, P], F32, name="w_t", tag="w_t")
            words = w_rows[c][:].bitcast(F32)
            for j in range(WORDS):
                nc.tensor.transpose(w_t[:, j, :], words[:, j * P : (j + 1) * P], identity[:])
            if c < STREAM_WARM_UP:
                nc.tensor.matmul(
                    out=idle_bank[:], lhsT=identity[:], rhs=identity[:], start=True, stop=True
                )
            grouped = grouped_pool.tile(
                [P, PASSES, P, PACK], BF16, name="grouped", tag="grouped", align_bytes=64
            )
            nc.scalar.copy(
                out=grouped[:].bitcast(F32),
                in_=w_t[:].rearrange("p (s u) o -> p s o u", u=2),
            )
            w_grouped[c] = grouped

        def quantise_chunk(c):
            nc.vector.quantize_mx(
                out=w_codes[:, c, :].bitcast(FP8X4),
                scales=w_scales[:, c, :],
                in_=w_grouped[c][:].rearrange("p s o t -> p (s o t)"),
            )

        for c in range(HEAD_CHUNKS):
            transpose_chunk(c)

        inv_rms_t = psum_misc.tile([P, P], F32, tag="bank")
        nc.tensor.transpose(inv_rms_t[:], inv_rms[:, 0:1].to_broadcast([P, P]), identity[:])
        h_grouped = keep.tile([P, PASSES, P, PACK], BF16, align_bytes=64)
        nc.vector.tensor_tensor(
            out=h_grouped[:],
            in0=xg[:],
            in1=inv_rms_t[:].unsqueeze(1).unsqueeze(3).to_broadcast([P, PASSES, P, PACK]),
            op=ALU.mult,
        )
        h_codes = keep.tile([P, PASSES * P], U32, align_bytes=64)
        h_scales = keep.tile([P, PASSES * P], U8, align_bytes=64)
        nc.vector.quantize_mx(
            out=h_codes[:].bitcast(FP8X4),
            scales=h_scales[:],
            in_=h_grouped[:].rearrange("p s r t -> p (s r t)"),
        )

        for c in range(HEAD_CHUNKS):
            quantise_chunk(c)
        for c in range(HEAD_CHUNKS, CHUNKS):
            transpose_chunk(c)
            quantise_chunk(c)

        out_sb = keep.tile([P, E], F32)
        for pair in range(E // PAIR):
            acc = psum_misc.tile([P, PAIR], F32, tag="bank")
            for half in range(2):
                c = 2 * pair + half
                for s in range(PASSES):
                    k_cols = slice(s * P, (s + 1) * P)
                    nc.tensor.matmul_mx(
                        out=acc[:, half * P : (half + 1) * P],
                        lhsT=h_codes[:, k_cols].bitcast(FP8X4),
                        lhsT_scale=h_scales[:, k_cols],
                        rhs=w_codes[:, c, k_cols].bitcast(FP8X4),
                        rhs_scale=w_scales[:, c, k_cols],
                        start=(s == 0),
                        stop=(s == PASSES - 1),
                    )
            cols = slice(pair * PAIR, (pair + 1) * PAIR)
            if pair == E // PAIR - 1:
                nc.vector.tensor_copy(out=out_sb[:, cols], in_=acc[:])
            else:
                nc.scalar.copy(out=out_sb[:, cols], in_=acc[:])
            nc.sync.dma_start(out=out_dram[:, cols], in_=out_sb[:, cols])
